import numpy as np
import ml_dtypes

BF16 = ml_dtypes.bfloat16


def bf(x):
    return np.asarray(x, np.float32).astype(BF16)


def f32(x):
    return np.asarray(x, np.float32)


def f64(x):
    return np.asarray(x).astype(np.float64)


def striped(idx):
    return np.tile(idx.reshape(-1, 16).T, (8, 1))


C, S, N, T = 512, 1024, 512, 8
LAM = 1.0507009873554804934193349852946
ALPHA = 1.6732632423543772848170429916717


def setup_inputs():
    return {"tok": bf(np.random.standard_normal((C, N, T))), "w": bf(np.random.standard_normal((C, C)) * np.sqrt(T / C)), "b": f32(0.1 * np.random.standard_normal((C, 1))), "base": f32(np.random.standard_normal((C, S))), "offs": striped(np.random.permutation(S)[:N])}


def reference(tok, w, b, base, offs):
    idx = offs[:16].T.reshape(-1)
    mean = f64(tok).sum(axis=-1) / T
    v = f64(w).T @ mean + f64(b)
    pos = LAM * np.maximum(v, 0.0)
    neg = LAM * ALPHA * (np.exp(np.minimum(v, 0.0)) - 1.0)
    out = f64(base).copy()
    out[:, idx] = pos + neg
    return out

@@ -1,0 +1,71 @@
+import concourse.mybir as mybir
+
+BF16, F32, U16 = mybir.dt.bfloat16, mybir.dt.float32, mybir.dt.uint16
+ADD, MULT = mybir.AluOpType.add, mybir.AluOpType.mult
+RELU, EXP = mybir.ActivationFunctionType.Relu, mybir.ActivationFunctionType.Exp
+
+P = 128
+C, S, N, T = 512, 1024, 512, 8
+BLOCKS = C // P
+LAM = 1.0507009873554804934193349852946
+ALPHA = 1.6732632423543772848170429916717
+
+FLOPS = 2 * C * C * N
+
+
+def tile_hierarchicaljointmodeldan_kernel(tc, tok, w, b, base, offs, out):
+    nc = tc.nc
+    with (
+        tc.tile_pool(name="held", bufs=1) as held,
+        tc.tile_pool(name="work", bufs=2) as work,
+        tc.psum_pool(name="psum", bufs=1) as psum,
+    ):
+        offsets = held.tile([P, N // 16], U16, name="offsets")
+        nc.sync.dma_start(offsets[:], offs)
+
+        tokens = [held.tile([P, N, T], BF16, name=f"tokens{kb}") for kb in range(BLOCKS)]
+        weights = held.tile([P, BLOCKS, C], BF16, name="weights")
+        nc.sync.dma_start(tokens[0][:], tok[0:P])
+        nc.sync.dma_start(weights[:], w.rearrange("(kb p) c -> p kb c", p=P))
+        for kb in range(1, BLOCKS):
+            nc.sync.dma_start(tokens[kb][:], tok[kb * P : (kb + 1) * P])
+
+        windows = [held.tile([P, S], F32, name=f"window{cb}") for cb in range(BLOCKS)]
+        for cb in range(BLOCKS):
+            nc.sync.dma_start(windows[cb][:], base[cb * P : (cb + 1) * P])
+
+        bias = held.tile([P, BLOCKS], F32, name="bias")
+        with nc.allow_non_contiguous_dma(reason="512 floats, one to a partition and column"):
+            nc.scalar.dma_start(bias[:], b.rearrange("(cb p) one -> p (cb one)", p=P))
+        lam_bias = held.tile([P, BLOCKS], F32, name="lam_bias")
+        nc.vector.tensor_scalar_mul(lam_bias[:], bias[:], LAM)
+        minus_bias = held.tile([P, BLOCKS], F32, name="minus_bias")
+        nc.vector.tensor_scalar_mul(minus_bias[:], bias[:], -1.0)
+
+        sums = [held.tile([P, N], BF16, name=f"sums{kb}") for kb in range(BLOCKS)]
+        for kb in range(BLOCKS):
+            with nc.allow_low_precision(reason="float32 sum of 8, rounded once to bfloat16"):
+                nc.vector.tensor_reduce(sums[kb][:], tokens[kb][:], mybir.AxisListType.X, ADD)
+
+        for cb in range(BLOCKS):
+            product = psum.tile([P, N], F32, name=f"product{cb}")
+            for kb in range(BLOCKS):
+                nc.tensor.matmul(
+                    product[:],
+                    weights[:, kb, cb * P : (cb + 1) * P],
+                    sums[kb][:],
+                    start=(kb == 0),
+                    stop=(kb == BLOCKS - 1),
+                )
+
+            pos = work.tile([P, N], F32, name="pos")
+            nc.scalar.activation(pos[:], product[:], RELU, bias=lam_bias[:, cb : cb + 1], scale=LAM / T)
+            depth = work.tile([P, N], F32, name="depth")
+            nc.scalar.activation(depth[:], product[:], RELU, bias=minus_bias[:, cb : cb + 1], scale=-1.0 / T)
+            decay = work.tile([P, N], F32, name="decay")
+            nc.scalar.activation(decay[:], depth[:], EXP, scale=-1.0)
+            neg = work.tile([P, N], F32, name="neg")
+            nc.gpsimd.tensor_scalar(neg[:], decay[:], -1.0, LAM * ALPHA, op0=ADD, op1=MULT)
+
+            nc.vector.tensor_tensor(windows[cb][:].indirect(offsets[:]), pos[:], neg[:], ADD)
+            nc.sync.dma_start(out[cb * P : (cb + 1) * P], windows[cb][:])

@@ -1,12 +1,18 @@
 import concourse.mybir as mybir
+from concourse.masks import make_identity
 
 BF16, F32, U16 = mybir.dt.bfloat16, mybir.dt.float32, mybir.dt.uint16
 ADD, MULT = mybir.AluOpType.add, mybir.AluOpType.mult
-RELU, EXP = mybir.ActivationFunctionType.Relu, mybir.ActivationFunctionType.Exp
+RELU, EXP, COPY = (
+    mybir.ActivationFunctionType.Relu,
+    mybir.ActivationFunctionType.Exp,
+    mybir.ActivationFunctionType.Copy,
+)
 
 P = 128
 C, S, N, T = 512, 1024, 512, 8
 BLOCKS = C // P
+HALF = N // 2
 LAM = 1.0507009873554804934193349852946
 ALPHA = 1.6732632423543772848170429916717
 
@@ -19,16 +25,19 @@ def tile_hierarchicaljointmodeldan_kernel(tc, tok, w, b, base, offs, out):
         tc.tile_pool(name="held", bufs=1) as held,
         tc.tile_pool(name="work", bufs=2) as work,
         tc.psum_pool(name="psum", bufs=1) as psum,
+        tc.psum_pool(name="psum_ring", bufs=2) as psum_ring,
     ):
         offsets = held.tile([P, N // 16], U16, name="offsets")
         nc.sync.dma_start(offsets[:], offs)
 
-        tokens = [held.tile([P, N, T], BF16, name=f"tokens{kb}") for kb in range(BLOCKS)]
+        first = [held.tile([P, HALF, T], BF16, name=f"first{kb}") for kb in range(BLOCKS)]
+        second = [held.tile([P, HALF, T], BF16, name=f"second{kb}") for kb in range(BLOCKS)]
         weights = held.tile([P, BLOCKS, C], BF16, name="weights")
-        nc.sync.dma_start(tokens[0][:], tok[0:P])
-        nc.sync.dma_start(weights[:], w.rearrange("(kb p) c -> p kb c", p=P))
-        for kb in range(1, BLOCKS):
-            nc.sync.dma_start(tokens[kb][:], tok[kb * P : (kb + 1) * P])
+        for kb in range(BLOCKS):
+            nc.sync.dma_start(first[kb][:], tok[kb * P : (kb + 1) * P, 0:HALF])
+            nc.sync.dma_start(second[kb][:], tok[kb * P : (kb + 1) * P, HALF:N])
+            if kb == 0:
+                nc.sync.dma_start(weights[:], w.rearrange("(kb p) c -> p kb c", p=P))
 
         windows = [held.tile([P, S], F32, name=f"window{cb}") for cb in range(BLOCKS)]
         for cb in range(BLOCKS):
@@ -42,22 +51,30 @@ def tile_hierarchicaljointmodeldan_kernel(tc, tok, w, b, base, offs, out):
         minus_bias = held.tile([P, BLOCKS], F32, name="minus_bias")
         nc.vector.tensor_scalar_mul(minus_bias[:], bias[:], -1.0)
 
+        identity = held.tile([P, P], BF16, name="identity")
+        make_identity(nc, identity[:])
+
         sums = [held.tile([P, N], BF16, name=f"sums{kb}") for kb in range(BLOCKS)]
+        products = [psum.tile([P, N], F32, name=f"product{cb}") for cb in range(BLOCKS)]
         for kb in range(BLOCKS):
             with nc.allow_low_precision(reason="float32 sum of 8, rounded once to bfloat16"):
-                nc.vector.tensor_reduce(sums[kb][:], tokens[kb][:], mybir.AxisListType.X, ADD)
+                nc.vector.tensor_reduce(sums[kb][:, 0:HALF], first[kb][:], mybir.AxisListType.X, ADD)
+            total = psum_ring.tile([P, HALF], F32, name="total")
+            for t in range(T):
+                nc.tensor.matmul(total[:], identity[:], second[kb][:, :, t], start=(t == 0), stop=(t == T - 1))
+            nc.scalar.activation(sums[kb][:, HALF:N], total[:], COPY)
 
-        for cb in range(BLOCKS):
-            product = psum.tile([P, N], F32, name=f"product{cb}")
-            for kb in range(BLOCKS):
+            for cb in range(BLOCKS):
                 nc.tensor.matmul(
-                    product[:],
+                    products[cb][:],
                     weights[:, kb, cb * P : (cb + 1) * P],
                     sums[kb][:],
                     start=(kb == 0),
                     stop=(kb == BLOCKS - 1),
                 )
 
+        for cb in range(BLOCKS):
+            product = products[cb]
             pos = work.tile([P, N], F32, name="pos")
             nc.scalar.activation(pos[:], product[:], RELU, bias=lam_bias[:, cb : cb + 1], scale=LAM / T)
             depth = work.tile([P, N], F32, name="depth")

@@ -3,11 +3,7 @@ from concourse.masks import make_identity
 
 BF16, F32, U16 = mybir.dt.bfloat16, mybir.dt.float32, mybir.dt.uint16
 ADD, MULT = mybir.AluOpType.add, mybir.AluOpType.mult
-RELU, EXP, COPY = (
-    mybir.ActivationFunctionType.Relu,
-    mybir.ActivationFunctionType.Exp,
-    mybir.ActivationFunctionType.Copy,
-)
+RELU, EXP = mybir.ActivationFunctionType.Relu, mybir.ActivationFunctionType.Exp
 
 P = 128
 C, S, N, T = 512, 1024, 512, 8
@@ -59,10 +55,11 @@ def tile_hierarchicaljointmodeldan_kernel(tc, tok, w, b, base, offs, out):
         for kb in range(BLOCKS):
             with nc.allow_low_precision(reason="float32 sum of 8, rounded once to bfloat16"):
                 nc.vector.tensor_reduce(sums[kb][:, 0:HALF], first[kb][:], mybir.AxisListType.X, ADD)
-            total = psum_ring.tile([P, HALF], F32, name="total")
-            for t in range(T):
-                nc.tensor.matmul(total[:], identity[:], second[kb][:, :, t], start=(t == 0), stop=(t == T - 1))
-            nc.scalar.activation(sums[kb][:, HALF:N], total[:], COPY)
+            pair = psum_ring.tile([P, HALF, 2], F32, name="pair")
+            for t in range(0, T, 2):
+                nc.tensor.matmul(pair[:], identity[:], second[kb][:, :, t : t + 2], start=(t == 0), stop=(t == T - 2))
+            with nc.allow_low_precision(reason="float32 sum of 8, rounded once to bfloat16"):
+                nc.vector.tensor_reduce(sums[kb][:, HALF:N], pair[:], mybir.AxisListType.X, ADD)
 
             for cb in range(BLOCKS):
                 nc.tensor.matmul(
@@ -75,12 +72,12 @@ def tile_hierarchicaljointmodeldan_kernel(tc, tok, w, b, base, offs, out):
 
         for cb in range(BLOCKS):
             product = products[cb]
-            pos = work.tile([P, N], F32, name="pos")
-            nc.scalar.activation(pos[:], product[:], RELU, bias=lam_bias[:, cb : cb + 1], scale=LAM / T)
             depth = work.tile([P, N], F32, name="depth")
             nc.scalar.activation(depth[:], product[:], RELU, bias=minus_bias[:, cb : cb + 1], scale=-1.0 / T)
             decay = work.tile([P, N], F32, name="decay")
             nc.scalar.activation(decay[:], depth[:], EXP, scale=-1.0)
+            pos = work.tile([P, N], F32, name="pos")
+            nc.scalar.activation(pos[:], product[:], RELU, bias=lam_bias[:, cb : cb + 1], scale=LAM / T)
             neg = work.tile([P, N], F32, name="neg")
             nc.gpsimd.tensor_scalar(neg[:], decay[:], -1.0, LAM * ALPHA, op0=ADD, op1=MULT)
 

@@ -4,15 +4,18 @@ from concourse.masks import make_identity
 BF16, F32, U16 = mybir.dt.bfloat16, mybir.dt.float32, mybir.dt.uint16
 ADD, MULT = mybir.AluOpType.add, mybir.AluOpType.mult
 RELU, EXP = mybir.ActivationFunctionType.Relu, mybir.ActivationFunctionType.Exp
+X = mybir.AxisListType.X
 
 P = 128
 C, S, N, T = 512, 1024, 512, 8
 BLOCKS = C // P
-HALF = N // 2
 LAM = 1.0507009873554804934193349852946
 ALPHA = 1.6732632423543772848170429916717
 
 FLOPS = 2 * C * C * N
+
+OWN, GROUP, GROUPS = 128, 192, 2
+assert OWN + GROUPS * GROUP == N
 
 
 def tile_hierarchicaljointmodeldan_kernel(tc, tok, w, b, base, offs, out):
@@ -20,20 +23,22 @@ def tile_hierarchicaljointmodeldan_kernel(tc, tok, w, b, base, offs, out):
     with (
         tc.tile_pool(name="held", bufs=1) as held,
         tc.tile_pool(name="work", bufs=2) as work,
-        tc.psum_pool(name="psum", bufs=1) as psum,
-        tc.psum_pool(name="psum_ring", bufs=2) as psum_ring,
+        tc.psum_pool(name="psum", bufs=2) as psum,
+        tc.psum_pool(name="psum_pairs", bufs=4) as psum_pairs,
     ):
         offsets = held.tile([P, N // 16], U16, name="offsets")
         nc.sync.dma_start(offsets[:], offs)
 
-        first = [held.tile([P, HALF, T], BF16, name=f"first{kb}") for kb in range(BLOCKS)]
-        second = [held.tile([P, HALF, T], BF16, name=f"second{kb}") for kb in range(BLOCKS)]
-        weights = held.tile([P, BLOCKS, C], BF16, name="weights")
+        own = [held.tile([P, OWN, T], BF16, name=f"own{kb}") for kb in range(BLOCKS)]
+        group = [[held.tile([P, GROUP, T], BF16, name=f"group{kb}_{g}") for g in range(GROUPS)] for kb in range(BLOCKS)]
         for kb in range(BLOCKS):
-            nc.sync.dma_start(first[kb][:], tok[kb * P : (kb + 1) * P, 0:HALF])
-            nc.sync.dma_start(second[kb][:], tok[kb * P : (kb + 1) * P, HALF:N])
-            if kb == 0:
-                nc.sync.dma_start(weights[:], w.rearrange("(kb p) c -> p kb c", p=P))
+            rows = tok[kb * P : (kb + 1) * P]
+            nc.sync.dma_start(own[kb][:], rows[:, 0:OWN])
+            for g in range(GROUPS):
+                nc.sync.dma_start(group[kb][g][:], rows[:, OWN + g * GROUP : OWN + (g + 1) * GROUP])
+
+        weights = held.tile([P, BLOCKS, C], BF16, name="weights")
+        nc.sync.dma_start(weights[:], w.rearrange("(kb p) c -> p kb c", p=P))
 
         windows = [held.tile([P, S], F32, name=f"window{cb}") for cb in range(BLOCKS)]
         for cb in range(BLOCKS):
@@ -51,27 +56,31 @@ def tile_hierarchicaljointmodeldan_kernel(tc, tok, w, b, base, offs, out):
         make_identity(nc, identity[:])
 
         sums = [held.tile([P, N], BF16, name=f"sums{kb}") for kb in range(BLOCKS)]
-        products = [psum.tile([P, N], F32, name=f"product{cb}") for cb in range(BLOCKS)]
         for kb in range(BLOCKS):
             with nc.allow_low_precision(reason="float32 sum of 8, rounded once to bfloat16"):
-                nc.vector.tensor_reduce(sums[kb][:, 0:HALF], first[kb][:], mybir.AxisListType.X, ADD)
-            pair = psum_ring.tile([P, HALF, 2], F32, name="pair")
-            for t in range(0, T, 2):
-                nc.tensor.matmul(pair[:], identity[:], second[kb][:, :, t : t + 2], start=(t == 0), stop=(t == T - 2))
-            with nc.allow_low_precision(reason="float32 sum of 8, rounded once to bfloat16"):
-                nc.vector.tensor_reduce(sums[kb][:, HALF:N], pair[:], mybir.AxisListType.X, ADD)
+                nc.vector.tensor_reduce(sums[kb][:, 0:OWN], own[kb][:], X, ADD)
+            for g in range(GROUPS):
+                pair = psum_pairs.tile([P, GROUP, 2], F32, name="pair")
+                for t in range(0, T, 2):
+                    nc.tensor.matmul(
+                        pair[:], identity[:], group[kb][g][:, :, t : t + 2], start=(t == 0), stop=(t == T - 2)
+                    )
+                with nc.allow_low_precision(reason="float32 sum of 8, rounded once to bfloat16"):
+                    nc.vector.tensor_reduce(
+                        sums[kb][:, OWN + g * GROUP : OWN + (g + 1) * GROUP], pair[:], X, ADD
+                    )
 
-            for cb in range(BLOCKS):
+        for cb in range(BLOCKS):
+            product = psum.tile([P, N], F32, name="product")
+            for kb in range(BLOCKS):
                 nc.tensor.matmul(
-                    products[cb][:],
+                    product[:],
                     weights[:, kb, cb * P : (cb + 1) * P],
                     sums[kb][:],
                     start=(kb == 0),
                     stop=(kb == BLOCKS - 1),
                 )
 
-        for cb in range(BLOCKS):
-            product = products[cb]
             depth = work.tile([P, N], F32, name="depth")
             nc.scalar.activation(depth[:], product[:], RELU, bias=minus_bias[:, cb : cb + 1], scale=-1.0 / T)
             decay = work.tile([P, N], F32, name="decay")

@@ -65,10 +65,11 @@ def tile_hierarchicaljointmodeldan_kernel(tc, tok, w, b, base, offs, out):
                     nc.tensor.matmul(
                         pair[:], identity[:], group[kb][g][:, :, t : t + 2], start=(t == 0), stop=(t == T - 2)
                     )
-                with nc.allow_low_precision(reason="float32 sum of 8, rounded once to bfloat16"):
-                    nc.vector.tensor_reduce(
-                        sums[kb][:, OWN + g * GROUP : OWN + (g + 1) * GROUP], pair[:], X, ADD
-                    )
+                odd = work.tile([P, GROUP], F32, name="odd")
+                nc.vector.tensor_copy(odd[:], pair[:, :, 1])
+                nc.vector.tensor_tensor(
+                    sums[kb][:, OWN + g * GROUP : OWN + (g + 1) * GROUP], pair[:, :, 0], odd[:], ADD
+                )
 
         for cb in range(BLOCKS):
             product = psum.tile([P, N], F32, name="product")

@@ -14,8 +14,8 @@ ALPHA = 1.6732632423543772848170429916717
 
 FLOPS = 2 * C * C * N
 
-OWN, GROUP, GROUPS = 128, 192, 2
-assert OWN + GROUPS * GROUP == N
+VEC, TEN, GPS = 208, 208, 96
+assert VEC + TEN + GPS == N
 
 
 def tile_hierarchicaljointmodeldan_kernel(tc, tok, w, b, base, offs, out):
@@ -24,18 +24,23 @@ def tile_hierarchicaljointmodeldan_kernel(tc, tok, w, b, base, offs, out):
         tc.tile_pool(name="held", bufs=1) as held,
         tc.tile_pool(name="work", bufs=2) as work,
         tc.psum_pool(name="psum", bufs=2) as psum,
-        tc.psum_pool(name="psum_pairs", bufs=4) as psum_pairs,
+        tc.psum_pool(name="psum_pairs", bufs=2) as psum_pairs,
     ):
         offsets = held.tile([P, N // 16], U16, name="offsets")
         nc.sync.dma_start(offsets[:], offs)
 
-        own = [held.tile([P, OWN, T], BF16, name=f"own{kb}") for kb in range(BLOCKS)]
-        group = [[held.tile([P, GROUP, T], BF16, name=f"group{kb}_{g}") for g in range(GROUPS)] for kb in range(BLOCKS)]
+        for_tensor = [held.tile([P, TEN, T], BF16, name=f"for_tensor{kb}") for kb in range(BLOCKS)]
+        for_gpsimd = [held.tile([P, GPS, T], BF16, name=f"for_gpsimd{kb}") for kb in range(BLOCKS)]
+        for_vector = [held.tile([P, VEC, T], BF16, name=f"for_vector{kb}") for kb in range(BLOCKS)]
         for kb in range(BLOCKS):
             rows = tok[kb * P : (kb + 1) * P]
-            nc.sync.dma_start(own[kb][:], rows[:, 0:OWN])
-            for g in range(GROUPS):
-                nc.sync.dma_start(group[kb][g][:], rows[:, OWN + g * GROUP : OWN + (g + 1) * GROUP])
+            nc.sync.dma_start(for_vector[kb][:], rows[:, 0:VEC])
+            nc.sync.dma_start(for_tensor[kb][:], rows[:, VEC : VEC + TEN])
+            nc.sync.dma_start(for_gpsimd[kb][:], rows[:, VEC + TEN : N])
+
+        bias = held.tile([P, BLOCKS], F32, name="bias")
+        with nc.allow_non_contiguous_dma(reason="512 floats, one to a partition and column"):
+            nc.sync.dma_start(bias[:], b.rearrange("(cb p) one -> p (cb one)", p=P))
 
         weights = held.tile([P, BLOCKS, C], BF16, name="weights")
         nc.sync.dma_start(weights[:], w.rearrange("(kb p) c -> p kb c", p=P))
@@ -44,32 +49,35 @@ def tile_hierarchicaljointmodeldan_kernel(tc, tok, w, b, base, offs, out):
         for cb in range(BLOCKS):
             nc.sync.dma_start(windows[cb][:], base[cb * P : (cb + 1) * P])
 
-        bias = held.tile([P, BLOCKS], F32, name="bias")
-        with nc.allow_non_contiguous_dma(reason="512 floats, one to a partition and column"):
-            nc.scalar.dma_start(bias[:], b.rearrange("(cb p) one -> p (cb one)", p=P))
-        lam_bias = held.tile([P, BLOCKS], F32, name="lam_bias")
-        nc.vector.tensor_scalar_mul(lam_bias[:], bias[:], LAM)
-        minus_bias = held.tile([P, BLOCKS], F32, name="minus_bias")
-        nc.vector.tensor_scalar_mul(minus_bias[:], bias[:], -1.0)
-
         identity = held.tile([P, P], BF16, name="identity")
         make_identity(nc, identity[:])
 
+        warm = held.tile([P, 1], F32, name="warm")
+        nc.vector.memset(warm[:], 0.0)
+        nc.scalar.activation(warm[:], warm[:], EXP)
+
         sums = [held.tile([P, N], BF16, name=f"sums{kb}") for kb in range(BLOCKS)]
         for kb in range(BLOCKS):
-            with nc.allow_low_precision(reason="float32 sum of 8, rounded once to bfloat16"):
-                nc.vector.tensor_reduce(sums[kb][:, 0:OWN], own[kb][:], X, ADD)
-            for g in range(GROUPS):
-                pair = psum_pairs.tile([P, GROUP, 2], F32, name="pair")
-                for t in range(0, T, 2):
-                    nc.tensor.matmul(
-                        pair[:], identity[:], group[kb][g][:, :, t : t + 2], start=(t == 0), stop=(t == T - 2)
-                    )
-                odd = work.tile([P, GROUP], F32, name="odd")
-                nc.vector.tensor_copy(odd[:], pair[:, :, 1])
-                nc.vector.tensor_tensor(
-                    sums[kb][:, OWN + g * GROUP : OWN + (g + 1) * GROUP], pair[:, :, 0], odd[:], ADD
+            pair = psum_pairs.tile([P, TEN, 2], F32, name="pair")
+            for t in range(0, T, 2):
+                nc.tensor.matmul(
+                    pair[:], identity[:], for_tensor[kb][:, :, t : t + 2], start=(t == 0), stop=(t == T - 2)
                 )
+
+            fours = work.tile([P, GPS, 4], F32, name="fours")
+            nc.gpsimd.tensor_tensor(fours[:], for_gpsimd[kb][:, :, 0:4], for_gpsimd[kb][:, :, 4:8], ADD)
+            twos = work.tile([P, GPS, 2], F32, name="twos")
+            nc.gpsimd.tensor_tensor(twos[:], fours[:, :, 0:2], fours[:, :, 2:4], ADD)
+            nc.gpsimd.tensor_tensor(sums[kb][:, VEC + TEN : N], twos[:, :, 0], twos[:, :, 1], ADD)
+
+            with nc.allow_low_precision(reason="float32 sum of 8, rounded once to bfloat16"):
+                nc.vector.tensor_reduce(sums[kb][:, 0:VEC], for_vector[kb][:], X, ADD)
+                nc.vector.tensor_reduce(sums[kb][:, VEC : VEC + TEN], pair[:], X, ADD)
+
+        lam_bias = held.tile([P, BLOCKS], F32, name="lam_bias")
+        nc.gpsimd.tensor_scalar_mul(lam_bias[:], bias[:], LAM)
+        minus_bias = held.tile([P, BLOCKS], F32, name="minus_bias")
+        nc.gpsimd.tensor_scalar_mul(minus_bias[:], bias[:], -1.0)
 
         for cb in range(BLOCKS):
             product = psum.tile([P, N], F32, name="product")

@@ -3,7 +3,11 @@ from concourse.masks import make_identity
 
 BF16, F32, U16 = mybir.dt.bfloat16, mybir.dt.float32, mybir.dt.uint16
 ADD, MULT = mybir.AluOpType.add, mybir.AluOpType.mult
-RELU, EXP = mybir.ActivationFunctionType.Relu, mybir.ActivationFunctionType.Exp
+RELU, EXP, COPY = (
+    mybir.ActivationFunctionType.Relu,
+    mybir.ActivationFunctionType.Exp,
+    mybir.ActivationFunctionType.Copy,
+)
 X = mybir.AxisListType.X
 
 P = 128
@@ -14,8 +18,8 @@ ALPHA = 1.6732632423543772848170429916717
 
 FLOPS = 2 * C * C * N
 
-VEC, TEN, GPS = 208, 208, 96
-assert VEC + TEN + GPS == N
+TEN, VEC, GPS = 224, 192, 96
+assert TEN + VEC + GPS == N
 
 
 def tile_hierarchicaljointmodeldan_kernel(tc, tok, w, b, base, offs, out):
@@ -25,25 +29,25 @@ def tile_hierarchicaljointmodeldan_kernel(tc, tok, w, b, base, offs, out):
         tc.tile_pool(name="work", bufs=2) as work,
         tc.psum_pool(name="psum", bufs=2) as psum,
         tc.psum_pool(name="psum_pairs", bufs=2) as psum_pairs,
+        tc.psum_pool(name="psum_bias", bufs=1) as psum_bias,
     ):
-        offsets = held.tile([P, N // 16], U16, name="offsets")
-        nc.sync.dma_start(offsets[:], offs)
+        bias_rows = held.tile([BLOCKS, P], F32, name="bias_rows")
+        nc.sync.dma_start(bias_rows[:], b.rearrange("(cb p) one -> cb (p one)", p=P))
 
         for_tensor = [held.tile([P, TEN, T], BF16, name=f"for_tensor{kb}") for kb in range(BLOCKS)]
         for_gpsimd = [held.tile([P, GPS, T], BF16, name=f"for_gpsimd{kb}") for kb in range(BLOCKS)]
         for_vector = [held.tile([P, VEC, T], BF16, name=f"for_vector{kb}") for kb in range(BLOCKS)]
         for kb in range(BLOCKS):
             rows = tok[kb * P : (kb + 1) * P]
-            nc.sync.dma_start(for_vector[kb][:], rows[:, 0:VEC])
-            nc.sync.dma_start(for_tensor[kb][:], rows[:, VEC : VEC + TEN])
-            nc.sync.dma_start(for_gpsimd[kb][:], rows[:, VEC + TEN : N])
-
-        bias = held.tile([P, BLOCKS], F32, name="bias")
-        with nc.allow_non_contiguous_dma(reason="512 floats, one to a partition and column"):
-            nc.sync.dma_start(bias[:], b.rearrange("(cb p) one -> p (cb one)", p=P))
+            nc.sync.dma_start(for_tensor[kb][:], rows[:, 0:TEN])
+            nc.sync.dma_start(for_vector[kb][:], rows[:, TEN : TEN + VEC])
+            nc.sync.dma_start(for_gpsimd[kb][:], rows[:, TEN + VEC : N])
 
         weights = held.tile([P, BLOCKS, C], BF16, name="weights")
         nc.sync.dma_start(weights[:], w.rearrange("(kb p) c -> p kb c", p=P))
+
+        offsets = held.tile([P, N // 16], U16, name="offsets")
+        nc.sync.dma_start(offsets[:], offs)
 
         windows = [held.tile([P, S], F32, name=f"window{cb}") for cb in range(BLOCKS)]
         for cb in range(BLOCKS):
@@ -55,6 +59,15 @@ def tile_hierarchicaljointmodeldan_kernel(tc, tok, w, b, base, offs, out):
         warm = held.tile([P, 1], F32, name="warm")
         nc.vector.memset(warm[:], 0.0)
         nc.scalar.activation(warm[:], warm[:], EXP)
+
+        corner = held.tile([BLOCKS, BLOCKS], F32, name="corner")
+        make_identity(nc, corner[:])
+        bias = psum_bias.tile([P, BLOCKS], F32, name="bias")
+        nc.tensor.matmul(bias[:], bias_rows[:], corner[:], start=True, stop=True)
+        lam_bias = held.tile([P, BLOCKS], F32, name="lam_bias")
+        nc.scalar.activation(lam_bias[:], bias[:], COPY, scale=LAM)
+        minus_bias = held.tile([P, BLOCKS], F32, name="minus_bias")
+        nc.scalar.activation(minus_bias[:], bias[:], COPY, scale=-1.0)
 
         sums = [held.tile([P, N], BF16, name=f"sums{kb}") for kb in range(BLOCKS)]
         for kb in range(BLOCKS):
@@ -68,16 +81,11 @@ def tile_hierarchicaljointmodeldan_kernel(tc, tok, w, b, base, offs, out):
             nc.gpsimd.tensor_tensor(fours[:], for_gpsimd[kb][:, :, 0:4], for_gpsimd[kb][:, :, 4:8], ADD)
             twos = work.tile([P, GPS, 2], F32, name="twos")
             nc.gpsimd.tensor_tensor(twos[:], fours[:, :, 0:2], fours[:, :, 2:4], ADD)
-            nc.gpsimd.tensor_tensor(sums[kb][:, VEC + TEN : N], twos[:, :, 0], twos[:, :, 1], ADD)
+            nc.gpsimd.tensor_tensor(sums[kb][:, TEN + VEC : N], twos[:, :, 0], twos[:, :, 1], ADD)
 
             with nc.allow_low_precision(reason="float32 sum of 8, rounded once to bfloat16"):
-                nc.vector.tensor_reduce(sums[kb][:, 0:VEC], for_vector[kb][:], X, ADD)
-                nc.vector.tensor_reduce(sums[kb][:, VEC : VEC + TEN], pair[:], X, ADD)
-
-        lam_bias = held.tile([P, BLOCKS], F32, name="lam_bias")
-        nc.gpsimd.tensor_scalar_mul(lam_bias[:], bias[:], LAM)
-        minus_bias = held.tile([P, BLOCKS], F32, name="minus_bias")
-        nc.gpsimd.tensor_scalar_mul(minus_bias[:], bias[:], -1.0)
+                nc.vector.tensor_reduce(sums[kb][:, TEN : TEN + VEC], for_vector[kb][:], X, ADD)
+                nc.vector.tensor_reduce(sums[kb][:, 0:TEN], pair[:], X, ADD)
 
         for cb in range(BLOCKS):
             product = psum.tile([P, N], F32, name="product")

import concourse.mybir as mybir
from concourse.masks import make_identity

BF16, F32, U16 = mybir.dt.bfloat16, mybir.dt.float32, mybir.dt.uint16
ADD, MULT = mybir.AluOpType.add, mybir.AluOpType.mult
RELU, EXP, COPY = (
    mybir.ActivationFunctionType.Relu,
    mybir.ActivationFunctionType.Exp,
    mybir.ActivationFunctionType.Copy,
)
X = mybir.AxisListType.X

P = 128
C, S, N, T = 512, 1024, 512, 8
BLOCKS = C // P
LAM = 1.0507009873554804934193349852946
ALPHA = 1.6732632423543772848170429916717

FLOPS = 2 * C * C * N

TEN, VEC, GPS = 224, 192, 96
assert TEN + VEC + GPS == N


def tile_hierarchicaljointmodeldan_kernel(tc, tok, w, b, base, offs, out):
    nc = tc.nc
    with (
        tc.tile_pool(name="held", bufs=1) as held,
        tc.tile_pool(name="work", bufs=2) as work,
        tc.psum_pool(name="psum", bufs=2) as psum,
        tc.psum_pool(name="psum_pairs", bufs=2) as psum_pairs,
        tc.psum_pool(name="psum_bias", bufs=1) as psum_bias,
    ):
        bias_rows = held.tile([BLOCKS, P], F32, name="bias_rows")
        nc.sync.dma_start(bias_rows[:], b.rearrange("(cb p) one -> cb (p one)", p=P))

        for_tensor = [held.tile([P, TEN, T], BF16, name=f"for_tensor{kb}") for kb in range(BLOCKS)]
        for_gpsimd = [held.tile([P, GPS, T], BF16, name=f"for_gpsimd{kb}") for kb in range(BLOCKS)]
        for_vector = [held.tile([P, VEC, T], BF16, name=f"for_vector{kb}") for kb in range(BLOCKS)]
        for kb in range(BLOCKS):
            rows = tok[kb * P : (kb + 1) * P]
            nc.sync.dma_start(for_tensor[kb][:], rows[:, 0:TEN])
            nc.sync.dma_start(for_vector[kb][:], rows[:, TEN : TEN + VEC])
            nc.sync.dma_start(for_gpsimd[kb][:], rows[:, TEN + VEC : N])

        weights = held.tile([P, BLOCKS, C], BF16, name="weights")
        nc.sync.dma_start(weights[:], w.rearrange("(kb p) c -> p kb c", p=P))

        offsets = held.tile([P, N // 16], U16, name="offsets")
        nc.sync.dma_start(offsets[:], offs)

        windows = [held.tile([P, S], F32, name=f"window{cb}") for cb in range(BLOCKS)]
        for cb in range(BLOCKS):
            nc.sync.dma_start(windows[cb][:], base[cb * P : (cb + 1) * P])

        identity = held.tile([P, P], BF16, name="identity")
        make_identity(nc, identity[:])

        warm = held.tile([P, 1], F32, name="warm")
        nc.vector.memset(warm[:], 0.0)
        nc.scalar.activation(warm[:], warm[:], EXP)

        corner = held.tile([BLOCKS, BLOCKS], F32, name="corner")
        make_identity(nc, corner[:])
        bias = psum_bias.tile([P, BLOCKS], F32, name="bias")
        nc.tensor.matmul(bias[:], bias_rows[:], corner[:], start=True, stop=True)
        lam_bias = held.tile([P, BLOCKS], F32, name="lam_bias")
        nc.scalar.activation(lam_bias[:], bias[:], COPY, scale=LAM)
        minus_bias = held.tile([P, BLOCKS], F32, name="minus_bias")
        nc.scalar.activation(minus_bias[:], bias[:], COPY, scale=-1.0)

        sums = [held.tile([P, N], BF16, name=f"sums{kb}") for kb in range(BLOCKS)]
        for kb in range(BLOCKS):
            pair = psum_pairs.tile([P, TEN, 2], F32, name="pair")
            for t in range(0, T, 2):
                nc.tensor.matmul(
                    pair[:], identity[:], for_tensor[kb][:, :, t : t + 2], start=(t == 0), stop=(t == T - 2)
                )

            fours = work.tile([P, GPS, 4], F32, name="fours")
            nc.gpsimd.tensor_tensor(fours[:], for_gpsimd[kb][:, :, 0:4], for_gpsimd[kb][:, :, 4:8], ADD)
            twos = work.tile([P, GPS, 2], F32, name="twos")
            nc.gpsimd.tensor_tensor(twos[:], fours[:, :, 0:2], fours[:, :, 2:4], ADD)
            nc.gpsimd.tensor_tensor(sums[kb][:, TEN + VEC : N], twos[:, :, 0], twos[:, :, 1], ADD)

            with nc.allow_low_precision(reason="float32 sum of 8, rounded once to bfloat16"):
                nc.vector.tensor_reduce(sums[kb][:, TEN : TEN + VEC], for_vector[kb][:], X, ADD)
                nc.vector.tensor_reduce(sums[kb][:, 0:TEN], pair[:], X, ADD)

        for cb in range(BLOCKS):
            product = psum.tile([P, N], F32, name="product")
            for kb in range(BLOCKS):
                nc.tensor.matmul(
                    product[:],
                    weights[:, kb, cb * P : (cb + 1) * P],
                    sums[kb][:],
                    start=(kb == 0),
                    stop=(kb == BLOCKS - 1),
                )

            depth = work.tile([P, N], F32, name="depth")
            nc.scalar.activation(depth[:], product[:], RELU, bias=minus_bias[:, cb : cb + 1], scale=-1.0 / T)
            decay = work.tile([P, N], F32, name="decay")
            nc.scalar.activation(decay[:], depth[:], EXP, scale=-1.0)
            pos = work.tile([P, N], F32, name="pos")
            nc.scalar.activation(pos[:], product[:], RELU, bias=lam_bias[:, cb : cb + 1], scale=LAM / T)
            neg = work.tile([P, N], F32, name="neg")
            nc.gpsimd.tensor_scalar(neg[:], decay[:], -1.0, LAM * ALPHA, op0=ADD, op1=MULT)

            nc.vector.tensor_tensor(windows[cb][:].indirect(offsets[:]), pos[:], neg[:], ADD)
            nc.sync.dma_start(out[cb * P : (cb + 1) * P], windows[cb][:])
